import numpy as np
import ml_dtypes


def mxq(x, axis, fmt="e4m3"):
    dtype, down = {"e4m3": (ml_dtypes.float8_e4m3fn, 7), "e5m2": (ml_dtypes.float8_e5m2, 14)}[fmt]
    v = np.moveaxis(np.asarray(x, np.float32).astype(ml_dtypes.bfloat16).astype(np.float64), axis, -1)
    blocks = v.reshape(v.shape[:-1] + (-1, 32))
    amax = np.abs(blocks).max(-1, keepdims=True)
    byte = np.maximum(np.where(amax > 0, np.frexp(amax)[1] - 1 + 127, 0) - down, 1)
    scale = np.exp2(byte - 127.0)
    codes = (blocks / scale).astype(np.float32).astype(dtype).astype(np.float64)
    return np.moveaxis((codes * scale).reshape(v.shape), -1, axis)


WIDE = False


def mx_kscale(k):
    if not WIDE:
        return np.ones(k)
    levels = np.array([10, -10, 5, -5, 0])
    a = np.random.permutation(np.resize(levels, k // 512 * 4)).reshape(k // 512, 4)
    idx = np.arange(k)
    return np.exp2(a[idx // 512, idx % 128 // 32])


BF16 = ml_dtypes.bfloat16


def bf(x):
    return np.asarray(x, np.float32).astype(BF16)


def f64(x):
    return np.asarray(x).astype(np.float64)


E2M1 = np.array([0.0, 0.5, 1.0, 1.5, 2.0, 3.0, 4.0, 6.0, -0.0, -0.5, -1.0, -1.5, -2.0, -3.0, -4.0, -6.0])


def pack_weight(w, fmt):
    k, n = w.shape
    w = f64(bf(w)).reshape(k // 32, 32, n)
    amax = np.abs(w).max(1)
    if fmt == "e4m3":
        byte = np.frexp(amax)[1] - 1 + 127 - 7
    else:
        mant, ex = np.frexp(amax / 6.0)
        byte = np.where(mant > 0.5, ex, ex - 1) + 127
    byte = np.clip(np.where(amax > 0, byte, 1), 1, 254)
    scaled = (w * np.exp2(127.0 - byte)[:, None, :]).reshape(k, n).astype(np.float32)
    by_word = np.ascontiguousarray(scaled.reshape(k // 512, 128, 4, n).transpose(0, 1, 3, 2))
    if fmt == "e4m3":
        words = by_word.astype(ml_dtypes.float8_e4m3fn).view(np.uint8)
    else:
        c = by_word.astype(ml_dtypes.float4_e2m1fn).view(np.uint8) & 0xF
        words = c[..., 0::2] | (c[..., 1::2] << 4)
    return np.ascontiguousarray(words), np.ascontiguousarray(byte.astype(np.uint8).reshape(k // 512, 16, n))


def unpack_weight(words, scales, fmt):
    g, p, n, _ = words.shape
    if fmt == "e4m3":
        vals = np.ascontiguousarray(words).view(ml_dtypes.float8_e4m3fn).astype(np.float64)
    else:
        nib = np.empty((g, p, n, 4), np.uint8)
        nib[..., 0::2] = words & 0xF
        nib[..., 1::2] = words >> 4
        vals = E2M1[nib]
    vals = vals * np.repeat(np.exp2(scales.astype(np.float64) - 127.0), 8, axis=1)[..., None]
    return vals.transpose(0, 1, 3, 2).reshape(g * 512, n)


B, IN, OUT = 128, 4096, 2048


def setup_inputs():
    s = mx_kscale(IN)
    input_data = bf(np.random.standard_normal((B, IN)) * s)
    weight_words, weight_scales = pack_weight((np.random.standard_normal((OUT, IN)) / np.sqrt(IN) / s).T, "e4m3")
    return {"input_data": input_data,
            "weight_words": weight_words,
            "weight_scales": weight_scales,
            "bias": bf(np.random.standard_normal(OUT) * 0.5),
            "prev_grad": bf(np.random.standard_normal((OUT, IN)) / np.sqrt(IN) / s),
            "prev_bias_grad": bf(np.random.standard_normal(OUT) * 0.5),
            "lr_samples": bf(np.random.uniform(0.1, 1.0, B))}


def reference(input_data, weight_words, weight_scales, bias, prev_grad, prev_bias_grad, lr_samples):
    xq = mxq(f64(input_data), 1, "e4m3")
    base = (xq @ unpack_weight(weight_words, weight_scales, "e4m3")) + f64(bias)
    pert = (xq @ mxq(f64(prev_grad), 1, "e4m3").T) + f64(prev_bias_grad)
    return base - f64(lr_samples)[:, None] * pert

@@ -1,0 +1,249 @@
+from contextlib import ExitStack
+
+import concourse.mybir as mybir
+from concourse.masks import make_identity
+
+F32 = mybir.dt.float32
+BF16 = mybir.dt.bfloat16
+U32 = mybir.dt.uint32
+U8 = mybir.dt.uint8
+I32 = mybir.dt.int32
+FP8X4 = mybir.dt.float8_e4m3fn_x4
+ALU = mybir.AluOpType
+
+P = 128
+B = 128
+K = 4096
+N = 2048
+KG = K // 512
+ND = 8
+FLOPS = 2 * 2 * B * K * N
+
+
+def tile_optimizedlinear_w_kernel(
+    tc, input_data, weight_words, weight_scales, bias, prev_grad, prev_bias_grad, lr_samples, out
+):
+    nc = tc.nc
+    with ExitStack() as ctx:
+        const = ctx.enter_context(tc.tile_pool(name="const", bufs=1))
+        graw = ctx.enter_context(tc.tile_pool(name="graw", bufs=4))
+        grp = ctx.enter_context(tc.tile_pool(name="grp", bufs=3))
+        cod = ctx.enter_context(tc.tile_pool(name="cod", bufs=6))
+        wpool = ctx.enter_context(tc.tile_pool(name="wpool", bufs=1))
+        ps_t = ctx.enter_context(tc.psum_pool(name="ps_t", bufs=6))
+        ps_p = ctx.enter_context(tc.psum_pool(name="ps_p", bufs=2))
+        ctx.enter_context(tc.manual_schedule())
+
+        ident = const.tile([P, P], F32, name="ident")
+        make_identity(nc, ident[:])
+        coef = const.tile([P, P], BF16, name="coef")
+        nc.vector.memset(coef[:], 0.0)
+        nc.vector.memset(coef[32:64, :], -1.0)
+        rows = const.tile([P, N], BF16, name="rows")
+        nc.vector.memset(rows[:], 0.0)
+        pick = const.tile([P, 64], BF16, name="pick")
+        nc.vector.memset(pick[:], 0.0)
+        nc.vector.memset(pick[0:32, :], 1.0)
+        planes = const.tile([P, 2, N], U8, name="planes", align_bytes=64)
+        nc.vector.memset(planes[:].rearrange("p h n -> p (h n)").bitcast(I32), 0)
+        nc.scalar.dma_start(out=coef[0:1, :], in_=lr_samples.rearrange("(o b) -> o b", o=1))
+        nc.scalar.dma_start(out=rows[0:1, :], in_=prev_bias_grad.rearrange("(o n) -> o n", o=1))
+        nc.scalar.dma_start(out=rows[32:33, :], in_=bias.rearrange("(o n) -> o n", o=1))
+
+        x_sb = const.tile([P, K], BF16, name="x_sb")
+        nc.sync.dma_start(out=x_sb[:, 0 : K // 2], in_=input_data[:, 0 : K // 2])
+        nc.sync.dma_start(out=x_sb[:, K // 2 : K], in_=input_data[:, K // 2 : K])
+
+        g_rows = prev_grad.rearrange("(d i s) k -> d i (s k)", i=P, s=2)
+        g_split = prev_grad.rearrange("(d i s) k -> d i s k", i=P, s=2)
+        g_tiles = {}
+
+        def load_g(d):
+            g_sb = graw.tile([P, 2 * K], BF16, name="g_sb", tag="g_sb")
+            g_tiles[d] = g_sb
+            if d == 0:
+                halves = g_sb[:].rearrange("p (s k) -> p s k", s=2)
+                nc.sync.dma_start(out=halves[:, :, 0 : K // 2], in_=g_split[d][:, :, 0 : K // 2])
+                nc.sync.dma_start(out=halves[:, :, K // 2 : K], in_=g_split[d][:, :, K // 2 : K])
+            else:
+                nc.sync.dma_start(out=g_sb[:], in_=g_rows[d])
+
+        for d in range(4):
+            load_g(d)
+
+        w_tiles = {}
+
+        def load_w():
+            for h in range(2):
+                for q in range(4):
+                    nc.sync.dma_start(
+                        out=planes[32 * q : 32 * q + 16, h, :].bitcast(I32),
+                        in_=weight_scales[4 * h : 4 * h + 4, 4 * q : 4 * q + 4, :].bitcast(I32),
+                    )
+            for g in range(KG - 1):
+                w_sb = wpool.tile([P, N], U32, name="w_sb%d" % g, align_bytes=64)
+                w_tiles[g] = w_sb
+                nc.sync.dma_start(
+                    out=w_sb[:].bitcast(I32),
+                    in_=weight_words[g].rearrange("p n t -> p (n t)").bitcast(I32),
+                )
+            for nt in range(4):
+                w_last = wpool.tile([P, 512], U32, name="w_last%d" % nt, align_bytes=64)
+                w_tiles[(KG - 1, nt)] = w_last
+                nc.sync.dma_start(
+                    out=w_last[:].bitcast(I32),
+                    in_=weight_words[KG - 1][:, nt * 512 : (nt + 1) * 512, :]
+                    .rearrange("p n t -> p (n t)")
+                    .bitcast(I32),
+                )
+
+        x_words = x_sb[:].bitcast(F32)
+        xg = const.tile([P, K], BF16, name="xg", align_bytes=64)
+        xg_words = xg[:].bitcast(F32)
+        for b in range(4):
+            xt = ps_t.tile([P, 4, P], F32, name="xt", tag="t")
+            for g2 in range(2):
+                g = 2 * b + g2
+                for u in range(2):
+                    nc.tensor.transpose(
+                        xt[:, 2 * g2 + u, :], x_words[:, 256 * g + u : 256 * (g + 1) : 2], ident[:]
+                    )
+            dst = xg_words[:, 512 * b : 512 * (b + 1)].rearrange("p (g r u) -> p g r u", g=2, u=2)
+            src = xt[:].rearrange("p (g u) r -> p g r u", g=2)
+            if b % 2 == 0:
+                nc.scalar.copy(out=dst, in_=src)
+            else:
+                nc.vector.tensor_copy(out=dst, in_=src)
+        xq = const.tile([P, K // 4], U32, name="xq", align_bytes=64)
+        xs = const.tile([P, K // 4], U8, name="xs", align_bytes=64)
+
+        grouped = {}
+        codes = {}
+
+        def transposes(hh):
+            d, h = divmod(hh, 2)
+            g_words = g_tiles[d][:].bitcast(F32)
+            gr = grp.tile([P, 4096], BF16, name="gr", tag="gr", align_bytes=64)
+            grouped[hh] = gr
+            gr_words = gr[:].bitcast(F32)
+            for gl in range(4):
+                g = 4 * h + gl
+                bank = ps_t.tile([P, 4, P], F32, name="bank", tag="t")
+                for s in range(2):
+                    for u in range(2):
+                        first = s * (K // 2) + 256 * g + u
+                        nc.tensor.transpose(
+                            bank[:, 2 * s + u, :], g_words[:, first : first + 255 : 2], ident[:]
+                        )
+                dst = gr_words[:, 512 * gl : 512 * (gl + 1)].rearrange("p (i c) -> p i c", c=4)
+                src = bank[:].rearrange("p c i -> p i c")
+                if gl < 3:
+                    nc.scalar.copy(out=dst, in_=src)
+                else:
+                    nc.vector.tensor_copy(out=dst, in_=src)
+
+        def quantise(hh):
+            cd = cod.tile([P, 1024], U32, name="cd", tag="cd", align_bytes=64)
+            sc = cod.tile([P, 1024], U8, name="sc", tag="sc", align_bytes=64)
+            codes[hh] = (cd, sc)
+            nc.vector.quantize_mx(out=cd[:].bitcast(FP8X4), scales=sc[:], in_=grouped[hh][:])
+
+        pert = {}
+
+        def pert_passes(d):
+            nt, half = divmod(d, 2)
+            if half == 0:
+                acc = ps_p.tile([P, 512], F32, name="acc", tag="acc")
+                pert[nt] = acc
+            acc = pert[nt]
+            for g in range(KG):
+                cd, sc = codes[2 * d + g // 4]
+                cols = slice(256 * (g % 4), 256 * (g % 4) + 256)
+                nc.tensor.matmul_mx(
+                    out=acc[:, 256 * half : 256 * half + 256],
+                    lhsT=xq[:, P * g : P * (g + 1)].bitcast(FP8X4),
+                    lhsT_scale=xs[:, P * g : P * (g + 1)],
+                    rhs=cd[:, cols].bitcast(FP8X4),
+                    rhs_scale=sc[:, cols],
+                    start=(g == 0),
+                    stop=(g == KG - 1),
+                )
+
+        comb = const.tile([P, N], F32, name="comb")
+        lr_col = const.tile([P, 1], F32, name="lr_col")
+
+        def small_terms():
+            lp = ps_t.tile([P, 512], F32, name="lp", tag="t")
+            nc.tensor.matmul(lp[:, 0:64], lhsT=coef[:], rhs=pick[:], start=True, stop=True)
+            nc.vector.tensor_copy(out=lr_col[:], in_=lp[:, 0:1])
+            for nt in range(4):
+                cp = ps_t.tile([P, 512], F32, name="cp", tag="t")
+                cols = slice(512 * nt, 512 * (nt + 1))
+                nc.tensor.matmul(cp[:], lhsT=coef[:], rhs=rows[:, cols], start=True, stop=True)
+                if nt % 2 == 0:
+                    nc.scalar.copy(out=comb[:, cols], in_=cp[:])
+                else:
+                    nc.vector.tensor_copy(out=comb[:, cols], in_=cp[:])
+
+        def fold_pert(nt):
+            cols = slice(512 * nt, 512 * (nt + 1))
+            nc.vector.scalar_tensor_tensor(
+                out=comb[:, cols],
+                in0=pert[nt][:],
+                scalar=lr_col[:, 0:1],
+                in1=comb[:, cols],
+                op0=ALU.mult,
+                op1=ALU.add,
+            )
+
+        for hh in range(2 * ND):
+            d, h = divmod(hh, 2)
+            transposes(hh)
+            if hh == 0:
+                nc.vector.quantize_mx(out=xq[:].bitcast(FP8X4), scales=xs[:], in_=xg[:])
+            else:
+                quantise(hh - 1)
+            if h == 1:
+                if d == 0:
+                    small_terms()
+                else:
+                    pert_passes(d - 1)
+                    if d % 2 == 0:
+                        fold_pert((d - 2) // 2)
+                if d + 4 < ND:
+                    load_g(d + 4)
+                if d + 4 == ND - 1:
+                    load_w()
+        quantise(2 * ND - 1)
+
+        base = {}
+        for nt in range(4):
+            bt = ps_t.tile([P, 512], F32, name="bt", tag="t")
+            base[nt] = bt
+
+        def base_pass(g, nt):
+            if g < KG - 1:
+                rhs = w_tiles[g][:, 512 * nt : 512 * (nt + 1)]
+            else:
+                rhs = w_tiles[(g, nt)][:]
+            nc.tensor.matmul_mx(
+                out=base[nt][:],
+                lhsT=xq[:, P * g : P * (g + 1)].bitcast(FP8X4),
+                lhsT_scale=xs[:, P * g : P * (g + 1)],
+                rhs=rhs.bitcast(FP8X4),
+                rhs_scale=planes[4 * (g % 4) : P, g // 4, 512 * nt : 512 * (nt + 1)],
+                start=(g == 0),
+                stop=(g == KG - 1),
+            )
+
+        for g in range(KG - 1):
+            for nt in range(4):
+                base_pass(g, nt)
+            if g == 1:
+                pert_passes(ND - 1)
+                fold_pert(3)
+        for nt in range(4):
+            cols = slice(512 * nt, 512 * (nt + 1))
+            base_pass(KG - 1, nt)
+            nc.vector.tensor_tensor(out=comb[:, cols], in0=base[nt][:], in1=comb[:, cols], op=ALU.subtract)
+            nc.sync.dma_start(out=out[:, cols], in_=comb[:, cols])

@@ -28,7 +28,7 @@ def tile_optimizedlinear_w_kernel(
         const = ctx.enter_context(tc.tile_pool(name="const", bufs=1))
         graw = ctx.enter_context(tc.tile_pool(name="graw", bufs=4))
         grp = ctx.enter_context(tc.tile_pool(name="grp", bufs=3))
-        cod = ctx.enter_context(tc.tile_pool(name="cod", bufs=6))
+        cod = ctx.enter_context(tc.tile_pool(name="cod", bufs=10))
         wpool = ctx.enter_context(tc.tile_pool(name="wpool", bufs=1))
         ps_t = ctx.enter_context(tc.psum_pool(name="ps_t", bufs=6))
         ps_p = ctx.enter_context(tc.psum_pool(name="ps_p", bufs=2))
@@ -50,7 +50,7 @@ def tile_optimizedlinear_w_kernel(
         nc.scalar.dma_start(out=rows[0:1, :], in_=prev_bias_grad.rearrange("(o n) -> o n", o=1))
         nc.scalar.dma_start(out=rows[32:33, :], in_=bias.rearrange("(o n) -> o n", o=1))
 
-        x_sb = const.tile([P, K], BF16, name="x_sb")
+        x_sb = graw.tile([P, K], BF16, name="x_sb", tag="g_sb", align_bytes=64)
         nc.sync.dma_start(out=x_sb[:, 0 : K // 2], in_=input_data[:, 0 : K // 2])
         nc.sync.dma_start(out=x_sb[:, K // 2 : K], in_=input_data[:, K // 2 : K])
 
@@ -59,7 +59,7 @@ def tile_optimizedlinear_w_kernel(
         g_tiles = {}
 
         def load_g(d):
-            g_sb = graw.tile([P, 2 * K], BF16, name="g_sb", tag="g_sb")
+            g_sb = graw.tile([P, 2 * K], BF16, name="g_sb", tag="g_sb", align_bytes=64)
             g_tiles[d] = g_sb
             if d == 0:
                 halves = g_sb[:].rearrange("p (s k) -> p s k", s=2)
@@ -68,7 +68,7 @@ def tile_optimizedlinear_w_kernel(
             else:
                 nc.sync.dma_start(out=g_sb[:], in_=g_rows[d])
 
-        for d in range(4):
+        for d in range(3):
             load_g(d)
 
         w_tiles = {}
@@ -80,25 +80,28 @@ def tile_optimizedlinear_w_kernel(
                         out=planes[32 * q : 32 * q + 16, h, :].bitcast(I32),
                         in_=weight_scales[4 * h : 4 * h + 4, 4 * q : 4 * q + 4, :].bitcast(I32),
                     )
-            for g in range(KG - 1):
+            for g in range(4):
                 w_sb = wpool.tile([P, N], U32, name="w_sb%d" % g, align_bytes=64)
-                w_tiles[g] = w_sb
+                w_tiles[g] = w_sb[:]
+            for pair in range(2):
+                w_two = graw.tile([P, 2 * N], U32, name="w_two", tag="g_sb", align_bytes=64)
+                w_tiles[4 + 2 * pair] = w_two[:, 0:N]
+                w_tiles[5 + 2 * pair] = w_two[:, N : 2 * N]
+            for g in range(KG - 1):
                 nc.sync.dma_start(
-                    out=w_sb[:].bitcast(I32),
+                    out=w_tiles[g].bitcast(I32),
                     in_=weight_words[g].rearrange("p n t -> p (n t)").bitcast(I32),
                 )
             for nt in range(4):
-                w_last = wpool.tile([P, 512], U32, name="w_last%d" % nt, align_bytes=64)
-                w_tiles[(KG - 1, nt)] = w_last
                 nc.sync.dma_start(
-                    out=w_last[:].bitcast(I32),
+                    out=w_tiles[KG - 1][:, nt * 512 : (nt + 1) * 512].bitcast(I32),
                     in_=weight_words[KG - 1][:, nt * 512 : (nt + 1) * 512, :]
                     .rearrange("p n t -> p (n t)")
                     .bitcast(I32),
                 )
 
         x_words = x_sb[:].bitcast(F32)
-        xg = const.tile([P, K], BF16, name="xg", align_bytes=64)
+        xg = grp.tile([P, K], BF16, name="xg", tag="gr", align_bytes=64)
         xg_words = xg[:].bitcast(F32)
         for b in range(4):
             xt = ps_t.tile([P, 4, P], F32, name="xt", tag="t")
@@ -203,18 +206,25 @@ def tile_optimizedlinear_w_kernel(
                 nc.vector.quantize_mx(out=xq[:].bitcast(FP8X4), scales=xs[:], in_=xg[:])
             else:
                 quantise(hh - 1)
+            if hh == 0:
+                load_g(3)
             if h == 1:
                 if d == 0:
                     small_terms()
-                else:
-                    pert_passes(d - 1)
-                    if d % 2 == 0:
-                        fold_pert((d - 2) // 2)
+                if d == 4:
+                    for dd in range(4):
+                        pert_passes(dd)
+                        if dd % 2 == 1:
+                            fold_pert(dd // 2)
                 if d + 4 < ND:
                     load_g(d + 4)
-                if d + 4 == ND - 1:
+                if d == 5:
                     load_w()
         quantise(2 * ND - 1)
+        for dd in range(4, ND):
+            pert_passes(dd)
+            if dd % 2 == 1:
+                fold_pert(dd // 2)
 
         base = {}
         for nt in range(4):
@@ -222,10 +232,7 @@ def tile_optimizedlinear_w_kernel(
             base[nt] = bt
 
         def base_pass(g, nt):
-            if g < KG - 1:
-                rhs = w_tiles[g][:, 512 * nt : 512 * (nt + 1)]
-            else:
-                rhs = w_tiles[(g, nt)][:]
+            rhs = w_tiles[g][:, 512 * nt : 512 * (nt + 1)]
             nc.tensor.matmul_mx(
                 out=base[nt][:],
                 lhsT=xq[:, P * g : P * (g + 1)].bitcast(FP8X4),
@@ -239,9 +246,6 @@ def tile_optimizedlinear_w_kernel(
         for g in range(KG - 1):
             for nt in range(4):
                 base_pass(g, nt)
-            if g == 1:
-                pert_passes(ND - 1)
-                fold_pert(3)
         for nt in range(4):
             cols = slice(512 * nt, 512 * (nt + 1))
             base_pass(KG - 1, nt)

@@ -29,6 +29,7 @@ def tile_optimizedlinear_w_kernel(
         graw = ctx.enter_context(tc.tile_pool(name="graw", bufs=4))
         grp = ctx.enter_context(tc.tile_pool(name="grp", bufs=3))
         cod = ctx.enter_context(tc.tile_pool(name="cod", bufs=10))
+        spool = ctx.enter_context(tc.tile_pool(name="spool", bufs=2))
         wpool = ctx.enter_context(tc.tile_pool(name="wpool", bufs=1))
         ps_t = ctx.enter_context(tc.psum_pool(name="ps_t", bufs=6))
         ps_p = ctx.enter_context(tc.psum_pool(name="ps_p", bufs=2))
@@ -123,6 +124,19 @@ def tile_optimizedlinear_w_kernel(
         grouped = {}
         codes = {}
 
+        sorted_words = {}
+
+        def sort_words(d):
+            g_words = g_tiles[d][:].bitcast(F32)
+            srt = spool.tile([P, 2048], F32, name="srt", tag="srt")
+            sorted_words[d] = srt
+            for s in range(2):
+                first = s * (K // 2) + 1024
+                nc.vector.tensor_copy(
+                    out=srt[:, 1024 * s : 1024 * (s + 1)].rearrange("p (g u c) -> p g u c", g=4, u=2),
+                    in_=g_words[:, first : first + 1024].rearrange("p (g c u) -> p g u c", g=4, u=2),
+                )
+
         def transposes(hh):
             d, h = divmod(hh, 2)
             g_words = g_tiles[d][:].bitcast(F32)
@@ -134,13 +148,16 @@ def tile_optimizedlinear_w_kernel(
                 bank = ps_t.tile([P, 4, P], F32, name="bank", tag="t")
                 for s in range(2):
                     for u in range(2):
-                        first = s * (K // 2) + 256 * g + u
-                        nc.tensor.transpose(
-                            bank[:, 2 * s + u, :], g_words[:, first : first + 255 : 2], ident[:]
-                        )
+                        if h == 0:
+                            first = s * (K // 2) + 256 * g + u
+                            block = g_words[:, first : first + 255 : 2]
+                        else:
+                            first = 1024 * s + 256 * gl + 128 * u
+                            block = sorted_words[d][:, first : first + 128]
+                        nc.tensor.transpose(bank[:, 2 * s + u, :], block, ident[:])
                 dst = gr_words[:, 512 * gl : 512 * (gl + 1)].rearrange("p (i c) -> p i c", c=4)
                 src = bank[:].rearrange("p c i -> p i c")
-                if gl < 3:
+                if gl < 3 or h == 1:
                     nc.scalar.copy(out=dst, in_=src)
                 else:
                     nc.vector.tensor_copy(out=dst, in_=src)
@@ -201,10 +218,15 @@ def tile_optimizedlinear_w_kernel(
 
         for hh in range(2 * ND):
             d, h = divmod(hh, 2)
-            transposes(hh)
-            if hh == 0:
-                nc.vector.quantize_mx(out=xq[:].bitcast(FP8X4), scales=xs[:], in_=xg[:])
+            if h == 0:
+                sort_words(d)
+                if hh == 0:
+                    nc.vector.quantize_mx(out=xq[:].bitcast(FP8X4), scales=xs[:], in_=xg[:])
+                else:
+                    quantise(hh - 1)
+                transposes(hh)
             else:
+                transposes(hh)
                 quantise(hh - 1)
             if hh == 0:
                 load_g(3)

@@ -17,6 +17,8 @@ K = 4096
 N = 2048
 KG = K // 512
 ND = 8
+SORT_FROM = 5
+NS = KG - SORT_FROM
 FLOPS = 2 * 2 * B * K * N
 
 
@@ -28,7 +30,7 @@ def tile_optimizedlinear_w_kernel(
         const = ctx.enter_context(tc.tile_pool(name="const", bufs=1))
         graw = ctx.enter_context(tc.tile_pool(name="graw", bufs=4))
         grp = ctx.enter_context(tc.tile_pool(name="grp", bufs=3))
-        cod = ctx.enter_context(tc.tile_pool(name="cod", bufs=10))
+        cod = ctx.enter_context(tc.tile_pool(name="cod", bufs=8))
         spool = ctx.enter_context(tc.tile_pool(name="spool", bufs=2))
         wpool = ctx.enter_context(tc.tile_pool(name="wpool", bufs=1))
         ps_t = ctx.enter_context(tc.psum_pool(name="ps_t", bufs=6))
@@ -101,6 +103,24 @@ def tile_optimizedlinear_w_kernel(
                     .bitcast(I32),
                 )
 
+        comb = const.tile([P, N], F32, name="comb")
+        lr_col = const.tile([P, 1], F32, name="lr_col")
+
+        def small_terms():
+            lp = ps_t.tile([P, 512], F32, name="lp", tag="t")
+            nc.tensor.matmul(lp[:, 0:64], lhsT=coef[:], rhs=pick[:], start=True, stop=True)
+            nc.vector.tensor_copy(out=lr_col[:], in_=lp[:, 0:1])
+            for nt in range(4):
+                cp = ps_t.tile([P, 512], F32, name="cp", tag="t")
+                cols = slice(512 * nt, 512 * (nt + 1))
+                nc.tensor.matmul(cp[:], lhsT=coef[:], rhs=rows[:, cols], start=True, stop=True)
+                if nt % 2 == 0:
+                    nc.scalar.copy(out=comb[:, cols], in_=cp[:])
+                else:
+                    nc.vector.tensor_copy(out=comb[:, cols], in_=cp[:])
+
+        small_terms()
+
         x_words = x_sb[:].bitcast(F32)
         xg = grp.tile([P, K], BF16, name="xg", tag="gr", align_bytes=64)
         xg_words = xg[:].bitcast(F32)
@@ -128,13 +148,13 @@ def tile_optimizedlinear_w_kernel(
 
         def sort_words(d):
             g_words = g_tiles[d][:].bitcast(F32)
-            srt = spool.tile([P, 2048], F32, name="srt", tag="srt")
+            srt = spool.tile([P, 2 * NS * 256], F32, name="srt", tag="srt")
             sorted_words[d] = srt
             for s in range(2):
-                first = s * (K // 2) + 1024
+                first = s * (K // 2) + 256 * SORT_FROM
                 nc.vector.tensor_copy(
-                    out=srt[:, 1024 * s : 1024 * (s + 1)].rearrange("p (g u c) -> p g u c", g=4, u=2),
-                    in_=g_words[:, first : first + 1024].rearrange("p (g c u) -> p g u c", g=4, u=2),
+                    out=srt[:, NS * 256 * s : NS * 256 * (s + 1)].rearrange("p (g u c) -> p g u c", g=NS, u=2),
+                    in_=g_words[:, first : first + NS * 256].rearrange("p (g c u) -> p g u c", g=NS, u=2),
                 )
 
         def transposes(hh):
@@ -148,11 +168,11 @@ def tile_optimizedlinear_w_kernel(
                 bank = ps_t.tile([P, 4, P], F32, name="bank", tag="t")
                 for s in range(2):
                     for u in range(2):
-                        if h == 0:
+                        if g < SORT_FROM:
                             first = s * (K // 2) + 256 * g + u
                             block = g_words[:, first : first + 255 : 2]
                         else:
-                            first = 1024 * s + 256 * gl + 128 * u
+                            first = NS * 256 * s + 256 * (g - SORT_FROM) + 128 * u
                             block = sorted_words[d][:, first : first + 128]
                         nc.tensor.transpose(bank[:, 2 * s + u, :], block, ident[:])
                 dst = gr_words[:, 512 * gl : 512 * (gl + 1)].rearrange("p (i c) -> p i c", c=4)
@@ -189,22 +209,6 @@ def tile_optimizedlinear_w_kernel(
                     stop=(g == KG - 1),
                 )
 
-        comb = const.tile([P, N], F32, name="comb")
-        lr_col = const.tile([P, 1], F32, name="lr_col")
-
-        def small_terms():
-            lp = ps_t.tile([P, 512], F32, name="lp", tag="t")
-            nc.tensor.matmul(lp[:, 0:64], lhsT=coef[:], rhs=pick[:], start=True, stop=True)
-            nc.vector.tensor_copy(out=lr_col[:], in_=lp[:, 0:1])
-            for nt in range(4):
-                cp = ps_t.tile([P, 512], F32, name="cp", tag="t")
-                cols = slice(512 * nt, 512 * (nt + 1))
-                nc.tensor.matmul(cp[:], lhsT=coef[:], rhs=rows[:, cols], start=True, stop=True)
-                if nt % 2 == 0:
-                    nc.scalar.copy(out=comb[:, cols], in_=cp[:])
-                else:
-                    nc.vector.tensor_copy(out=comb[:, cols], in_=cp[:])
-
         def fold_pert(nt):
             cols = slice(512 * nt, 512 * (nt + 1))
             nc.vector.scalar_tensor_tensor(
@@ -231,22 +235,15 @@ def tile_optimizedlinear_w_kernel(
             if hh == 0:
                 load_g(3)
             if h == 1:
-                if d == 0:
-                    small_terms()
-                if d == 4:
-                    for dd in range(4):
-                        pert_passes(dd)
-                        if dd % 2 == 1:
-                            fold_pert(dd // 2)
+                if d >= 2 and d % 2 == 0:
+                    pert_passes(d - 2)
+                    pert_passes(d - 1)
+                    fold_pert((d - 2) // 2)
                 if d + 4 < ND:
                     load_g(d + 4)
                 if d == 5:
                     load_w()
         quantise(2 * ND - 1)
-        for dd in range(4, ND):
-            pert_passes(dd)
-            if dd % 2 == 1:
-                fold_pert(dd // 2)
 
         base = {}
         for nt in range(4):
@@ -265,9 +262,13 @@ def tile_optimizedlinear_w_kernel(
                 stop=(g == KG - 1),
             )
 
+        pert_passes(ND - 2)
         for g in range(KG - 1):
             for nt in range(4):
                 base_pass(g, nt)
+            if g == 2:
+                pert_passes(ND - 1)
+                fold_pert(3)
         for nt in range(4):
             cols = slice(512 * nt, 512 * (nt + 1))
             base_pass(KG - 1, nt)

@@ -17,8 +17,6 @@ K = 4096
 N = 2048
 KG = K // 512
 ND = 8
-SORT_FROM = 5
-NS = KG - SORT_FROM
 FLOPS = 2 * 2 * B * K * N
 
 
@@ -30,12 +28,10 @@ def tile_optimizedlinear_w_kernel(
         const = ctx.enter_context(tc.tile_pool(name="const", bufs=1))
         graw = ctx.enter_context(tc.tile_pool(name="graw", bufs=4))
         grp = ctx.enter_context(tc.tile_pool(name="grp", bufs=3))
-        cod = ctx.enter_context(tc.tile_pool(name="cod", bufs=8))
-        spool = ctx.enter_context(tc.tile_pool(name="spool", bufs=2))
+        cod = ctx.enter_context(tc.tile_pool(name="cod", bufs=6))
         wpool = ctx.enter_context(tc.tile_pool(name="wpool", bufs=1))
         ps_t = ctx.enter_context(tc.psum_pool(name="ps_t", bufs=6))
         ps_p = ctx.enter_context(tc.psum_pool(name="ps_p", bufs=2))
-        ctx.enter_context(tc.manual_schedule())
 
         ident = const.tile([P, P], F32, name="ident")
         make_identity(nc, ident[:])
@@ -53,7 +49,7 @@ def tile_optimizedlinear_w_kernel(
         nc.scalar.dma_start(out=rows[0:1, :], in_=prev_bias_grad.rearrange("(o n) -> o n", o=1))
         nc.scalar.dma_start(out=rows[32:33, :], in_=bias.rearrange("(o n) -> o n", o=1))
 
-        x_sb = graw.tile([P, K], BF16, name="x_sb", tag="g_sb", align_bytes=64)
+        x_sb = const.tile([P, K], BF16, name="x_sb")
         nc.sync.dma_start(out=x_sb[:, 0 : K // 2], in_=input_data[:, 0 : K // 2])
         nc.sync.dma_start(out=x_sb[:, K // 2 : K], in_=input_data[:, K // 2 : K])
 
@@ -62,7 +58,7 @@ def tile_optimizedlinear_w_kernel(
         g_tiles = {}
 
         def load_g(d):
-            g_sb = graw.tile([P, 2 * K], BF16, name="g_sb", tag="g_sb", align_bytes=64)
+            g_sb = graw.tile([P, 2 * K], BF16, name="g_sb", tag="g_sb")
             g_tiles[d] = g_sb
             if d == 0:
                 halves = g_sb[:].rearrange("p (s k) -> p s k", s=2)
@@ -71,7 +67,7 @@ def tile_optimizedlinear_w_kernel(
             else:
                 nc.sync.dma_start(out=g_sb[:], in_=g_rows[d])
 
-        for d in range(3):
+        for d in range(4):
             load_g(d)
 
         w_tiles = {}
@@ -83,46 +79,25 @@ def tile_optimizedlinear_w_kernel(
                         out=planes[32 * q : 32 * q + 16, h, :].bitcast(I32),
                         in_=weight_scales[4 * h : 4 * h + 4, 4 * q : 4 * q + 4, :].bitcast(I32),
                     )
-            for g in range(4):
-                w_sb = wpool.tile([P, N], U32, name="w_sb%d" % g, align_bytes=64)
-                w_tiles[g] = w_sb[:]
-            for pair in range(2):
-                w_two = graw.tile([P, 2 * N], U32, name="w_two", tag="g_sb", align_bytes=64)
-                w_tiles[4 + 2 * pair] = w_two[:, 0:N]
-                w_tiles[5 + 2 * pair] = w_two[:, N : 2 * N]
             for g in range(KG - 1):
+                w_sb = wpool.tile([P, N], U32, name="w_sb%d" % g, align_bytes=64)
+                w_tiles[g] = w_sb
                 nc.sync.dma_start(
-                    out=w_tiles[g].bitcast(I32),
+                    out=w_sb[:].bitcast(I32),
                     in_=weight_words[g].rearrange("p n t -> p (n t)").bitcast(I32),
                 )
             for nt in range(4):
+                w_last = wpool.tile([P, 512], U32, name="w_last%d" % nt, align_bytes=64)
+                w_tiles[(KG - 1, nt)] = w_last
                 nc.sync.dma_start(
-                    out=w_tiles[KG - 1][:, nt * 512 : (nt + 1) * 512].bitcast(I32),
+                    out=w_last[:].bitcast(I32),
                     in_=weight_words[KG - 1][:, nt * 512 : (nt + 1) * 512, :]
                     .rearrange("p n t -> p (n t)")
                     .bitcast(I32),
                 )
 
-        comb = const.tile([P, N], F32, name="comb")
-        lr_col = const.tile([P, 1], F32, name="lr_col")
-
-        def small_terms():
-            lp = ps_t.tile([P, 512], F32, name="lp", tag="t")
-            nc.tensor.matmul(lp[:, 0:64], lhsT=coef[:], rhs=pick[:], start=True, stop=True)
-            nc.vector.tensor_copy(out=lr_col[:], in_=lp[:, 0:1])
-            for nt in range(4):
-                cp = ps_t.tile([P, 512], F32, name="cp", tag="t")
-                cols = slice(512 * nt, 512 * (nt + 1))
-                nc.tensor.matmul(cp[:], lhsT=coef[:], rhs=rows[:, cols], start=True, stop=True)
-                if nt % 2 == 0:
-                    nc.scalar.copy(out=comb[:, cols], in_=cp[:])
-                else:
-                    nc.vector.tensor_copy(out=comb[:, cols], in_=cp[:])
-
-        small_terms()
-
         x_words = x_sb[:].bitcast(F32)
-        xg = grp.tile([P, K], BF16, name="xg", tag="gr", align_bytes=64)
+        xg = const.tile([P, K], BF16, name="xg", align_bytes=64)
         xg_words = xg[:].bitcast(F32)
         for b in range(4):
             xt = ps_t.tile([P, 4, P], F32, name="xt", tag="t")
@@ -144,19 +119,6 @@ def tile_optimizedlinear_w_kernel(
         grouped = {}
         codes = {}
 
-        sorted_words = {}
-
-        def sort_words(d):
-            g_words = g_tiles[d][:].bitcast(F32)
-            srt = spool.tile([P, 2 * NS * 256], F32, name="srt", tag="srt")
-            sorted_words[d] = srt
-            for s in range(2):
-                first = s * (K // 2) + 256 * SORT_FROM
-                nc.vector.tensor_copy(
-                    out=srt[:, NS * 256 * s : NS * 256 * (s + 1)].rearrange("p (g u c) -> p g u c", g=NS, u=2),
-                    in_=g_words[:, first : first + NS * 256].rearrange("p (g c u) -> p g u c", g=NS, u=2),
-                )
-
         def transposes(hh):
             d, h = divmod(hh, 2)
             g_words = g_tiles[d][:].bitcast(F32)
@@ -168,16 +130,13 @@ def tile_optimizedlinear_w_kernel(
                 bank = ps_t.tile([P, 4, P], F32, name="bank", tag="t")
                 for s in range(2):
                     for u in range(2):
-                        if g < SORT_FROM:
-                            first = s * (K // 2) + 256 * g + u
-                            block = g_words[:, first : first + 255 : 2]
-                        else:
-                            first = NS * 256 * s + 256 * (g - SORT_FROM) + 128 * u
-                            block = sorted_words[d][:, first : first + 128]
-                        nc.tensor.transpose(bank[:, 2 * s + u, :], block, ident[:])
+                        first = s * (K // 2) + 256 * g + u
+                        nc.tensor.transpose(
+                            bank[:, 2 * s + u, :], g_words[:, first : first + 255 : 2], ident[:]
+                        )
                 dst = gr_words[:, 512 * gl : 512 * (gl + 1)].rearrange("p (i c) -> p i c", c=4)
                 src = bank[:].rearrange("p c i -> p i c")
-                if gl < 3 or h == 1:
+                if gl < 3:
                     nc.scalar.copy(out=dst, in_=src)
                 else:
                     nc.vector.tensor_copy(out=dst, in_=src)
@@ -209,6 +168,22 @@ def tile_optimizedlinear_w_kernel(
                     stop=(g == KG - 1),
                 )
 
+        comb = const.tile([P, N], F32, name="comb")
+        lr_col = const.tile([P, 1], F32, name="lr_col")
+
+        def small_terms():
+            lp = ps_t.tile([P, 512], F32, name="lp", tag="t")
+            nc.tensor.matmul(lp[:, 0:64], lhsT=coef[:], rhs=pick[:], start=True, stop=True)
+            nc.vector.tensor_copy(out=lr_col[:], in_=lp[:, 0:1])
+            for nt in range(4):
+                cp = ps_t.tile([P, 512], F32, name="cp", tag="t")
+                cols = slice(512 * nt, 512 * (nt + 1))
+                nc.tensor.matmul(cp[:], lhsT=coef[:], rhs=rows[:, cols], start=True, stop=True)
+                if nt % 2 == 0:
+                    nc.scalar.copy(out=comb[:, cols], in_=cp[:])
+                else:
+                    nc.vector.tensor_copy(out=comb[:, cols], in_=cp[:])
+
         def fold_pert(nt):
             cols = slice(512 * nt, 512 * (nt + 1))
             nc.vector.scalar_tensor_tensor(
@@ -222,26 +197,21 @@ def tile_optimizedlinear_w_kernel(
 
         for hh in range(2 * ND):
             d, h = divmod(hh, 2)
-            if h == 0:
-                sort_words(d)
-                if hh == 0:
-                    nc.vector.quantize_mx(out=xq[:].bitcast(FP8X4), scales=xs[:], in_=xg[:])
-                else:
-                    quantise(hh - 1)
-                transposes(hh)
-            else:
-                transposes(hh)
-                quantise(hh - 1)
+            transposes(hh)
             if hh == 0:
-                load_g(3)
+                nc.vector.quantize_mx(out=xq[:].bitcast(FP8X4), scales=xs[:], in_=xg[:])
+            else:
+                quantise(hh - 1)
             if h == 1:
-                if d >= 2 and d % 2 == 0:
-                    pert_passes(d - 2)
+                if d == 0:
+                    small_terms()
+                else:
                     pert_passes(d - 1)
-                    fold_pert((d - 2) // 2)
+                    if d % 2 == 0:
+                        fold_pert((d - 2) // 2)
                 if d + 4 < ND:
                     load_g(d + 4)
-                if d == 5:
+                if d + 4 == ND - 1:
                     load_w()
         quantise(2 * ND - 1)
 
@@ -251,7 +221,10 @@ def tile_optimizedlinear_w_kernel(
             base[nt] = bt
 
         def base_pass(g, nt):
-            rhs = w_tiles[g][:, 512 * nt : 512 * (nt + 1)]
+            if g < KG - 1:
+                rhs = w_tiles[g][:, 512 * nt : 512 * (nt + 1)]
+            else:
+                rhs = w_tiles[(g, nt)][:]
             nc.tensor.matmul_mx(
                 out=base[nt][:],
                 lhsT=xq[:, P * g : P * (g + 1)].bitcast(FP8X4),
@@ -262,11 +235,10 @@ def tile_optimizedlinear_w_kernel(
                 stop=(g == KG - 1),
             )
 
-        pert_passes(ND - 2)
         for g in range(KG - 1):
             for nt in range(4):
                 base_pass(g, nt)
-            if g == 2:
+            if g == 1:
                 pert_passes(ND - 1)
                 fold_pert(3)
         for nt in range(4):

@@ -32,6 +32,7 @@ def tile_optimizedlinear_w_kernel(
         wpool = ctx.enter_context(tc.tile_pool(name="wpool", bufs=1))
         ps_t = ctx.enter_context(tc.psum_pool(name="ps_t", bufs=6))
         ps_p = ctx.enter_context(tc.psum_pool(name="ps_p", bufs=2))
+        ctx.enter_context(tc.manual_schedule())
 
         ident = const.tile([P, P], F32, name="ident")
         make_identity(nc, ident[:])
@@ -58,16 +59,21 @@ def tile_optimizedlinear_w_kernel(
         g_tiles = {}
 
         def load_g(d):
-            g_sb = graw.tile([P, 2 * K], BF16, name="g_sb", tag="g_sb")
-            g_tiles[d] = g_sb
             if d == 0:
-                halves = g_sb[:].rearrange("p (s k) -> p s k", s=2)
-                nc.sync.dma_start(out=halves[:, :, 0 : K // 2], in_=g_split[d][:, :, 0 : K // 2])
-                nc.sync.dma_start(out=halves[:, :, K // 2 : K], in_=g_split[d][:, :, K // 2 : K])
+                for h in range(2):
+                    g_half = graw.tile([P, K], BF16, name="g_half", tag="g_sb")
+                    g_tiles[(d, h)] = (g_half, K // 4, 4 * h)
+                    nc.sync.dma_start(
+                        out=g_half[:].rearrange("p (s k) -> p s k", s=2),
+                        in_=g_split[d][:, :, h * (K // 2) : (h + 1) * (K // 2)],
+                    )
             else:
+                g_sb = graw.tile([P, 2 * K], BF16, name="g_sb", tag="g_sb")
+                for h in range(2):
+                    g_tiles[(d, h)] = (g_sb, K // 2, 0)
                 nc.sync.dma_start(out=g_sb[:], in_=g_rows[d])
 
-        for d in range(4):
+        for d in range(3):
             load_g(d)
 
         w_tiles = {}
@@ -121,7 +127,8 @@ def tile_optimizedlinear_w_kernel(
 
         def transposes(hh):
             d, h = divmod(hh, 2)
-            g_words = g_tiles[d][:].bitcast(F32)
+            g_sb, row_words, first_pass = g_tiles[(d, h)]
+            g_words = g_sb[:].bitcast(F32)
             gr = grp.tile([P, 4096], BF16, name="gr", tag="gr", align_bytes=64)
             grouped[hh] = gr
             gr_words = gr[:].bitcast(F32)
@@ -130,7 +137,7 @@ def tile_optimizedlinear_w_kernel(
                 bank = ps_t.tile([P, 4, P], F32, name="bank", tag="t")
                 for s in range(2):
                     for u in range(2):
-                        first = s * (K // 2) + 256 * g + u
+                        first = s * row_words + 256 * (g - first_pass) + u
                         nc.tensor.transpose(
                             bank[:, 2 * s + u, :], g_words[:, first : first + 255 : 2], ident[:]
                         )
@@ -202,6 +209,8 @@ def tile_optimizedlinear_w_kernel(
                 nc.vector.quantize_mx(out=xq[:].bitcast(FP8X4), scales=xs[:], in_=xg[:])
             else:
                 quantise(hh - 1)
+            if hh == 0:
+                load_g(3)
             if h == 1:
                 if d == 0:
                     small_terms()

@@ -58,6 +58,12 @@ def tile_optimizedlinear_w_kernel(
         g_split = prev_grad.rearrange("(d i s) k -> d i s k", i=P, s=2)
         g_tiles = {}
 
+        def load_scale_rows(h, q):
+            nc.sync.dma_start(
+                out=planes[32 * q : 32 * q + 16, h, :].bitcast(I32),
+                in_=weight_scales[4 * h : 4 * h + 4, 4 * q : 4 * q + 4, :].bitcast(I32),
+            )
+
         def load_g(d):
             if d == 0:
                 for h in range(2):
@@ -72,6 +78,9 @@ def tile_optimizedlinear_w_kernel(
                 for h in range(2):
                     g_tiles[(d, h)] = (g_sb, K // 2, 0)
                 nc.sync.dma_start(out=g_sb[:], in_=g_rows[d])
+            if 3 <= d <= 6:
+                for j in (2 * (d - 3), 2 * (d - 3) + 1):
+                    load_scale_rows(j // 4, j % 4)
 
         for d in range(3):
             load_g(d)
@@ -79,12 +88,6 @@ def tile_optimizedlinear_w_kernel(
         w_tiles = {}
 
         def load_w():
-            for h in range(2):
-                for q in range(4):
-                    nc.sync.dma_start(
-                        out=planes[32 * q : 32 * q + 16, h, :].bitcast(I32),
-                        in_=weight_scales[4 * h : 4 * h + 4, 4 * q : 4 * q + 4, :].bitcast(I32),
-                    )
             for g in range(KG - 1):
                 w_sb = wpool.tile([P, N], U32, name="w_sb%d" % g, align_bytes=64)
                 w_tiles[g] = w_sb

@@ -17,6 +17,9 @@ K = 4096
 N = 2048
 KG = K // 512
 ND = 8
+SORT_FROM = 6
+NS = KG - SORT_FROM
+VEC_BANKS = (3, 7)
 FLOPS = 2 * 2 * B * K * N
 
 
@@ -29,6 +32,7 @@ def tile_optimizedlinear_w_kernel(
         graw = ctx.enter_context(tc.tile_pool(name="graw", bufs=4))
         grp = ctx.enter_context(tc.tile_pool(name="grp", bufs=3))
         cod = ctx.enter_context(tc.tile_pool(name="cod", bufs=6))
+        spool = ctx.enter_context(tc.tile_pool(name="spool", bufs=2))
         wpool = ctx.enter_context(tc.tile_pool(name="wpool", bufs=1))
         ps_t = ctx.enter_context(tc.psum_pool(name="ps_t", bufs=6))
         ps_p = ctx.enter_context(tc.psum_pool(name="ps_p", bufs=2))
@@ -128,6 +132,20 @@ def tile_optimizedlinear_w_kernel(
         grouped = {}
         codes = {}
 
+        sorted_words = {}
+
+        def sort_words(d):
+            g_sb, row_words, first_pass = g_tiles[(d, 1)]
+            g_words = g_sb[:].bitcast(F32)
+            srt = spool.tile([P, 2 * NS * 256], F32, name="srt", tag="srt")
+            sorted_words[d] = srt
+            for s in range(2):
+                first = s * row_words + 256 * (SORT_FROM - first_pass)
+                nc.vector.tensor_copy(
+                    out=srt[:, NS * 256 * s : NS * 256 * (s + 1)].rearrange("p (g u c) -> p g u c", g=NS, u=2),
+                    in_=g_words[:, first : first + NS * 256].rearrange("p (g c u) -> p g u c", g=NS, u=2),
+                )
+
         def transposes(hh):
             d, h = divmod(hh, 2)
             g_sb, row_words, first_pass = g_tiles[(d, h)]
@@ -140,13 +158,16 @@ def tile_optimizedlinear_w_kernel(
                 bank = ps_t.tile([P, 4, P], F32, name="bank", tag="t")
                 for s in range(2):
                     for u in range(2):
-                        first = s * row_words + 256 * (g - first_pass) + u
-                        nc.tensor.transpose(
-                            bank[:, 2 * s + u, :], g_words[:, first : first + 255 : 2], ident[:]
-                        )
+                        if g < SORT_FROM:
+                            first = s * row_words + 256 * (g - first_pass) + u
+                            block = g_words[:, first : first + 255 : 2]
+                        else:
+                            first = NS * 256 * s + 256 * (g - SORT_FROM) + 128 * u
+                            block = sorted_words[d][:, first : first + 128]
+                        nc.tensor.transpose(bank[:, 2 * s + u, :], block, ident[:])
                 dst = gr_words[:, 512 * gl : 512 * (gl + 1)].rearrange("p (i c) -> p i c", c=4)
                 src = bank[:].rearrange("p c i -> p i c")
-                if gl < 3:
+                if g not in VEC_BANKS:
                     nc.scalar.copy(out=dst, in_=src)
                 else:
                     nc.vector.tensor_copy(out=dst, in_=src)
@@ -207,6 +228,8 @@ def tile_optimizedlinear_w_kernel(
 
         for hh in range(2 * ND):
             d, h = divmod(hh, 2)
+            if h == 0 and NS > 0:
+                sort_words(d)
             transposes(hh)
             if hh == 0:
                 nc.vector.quantize_mx(out=xq[:].bitcast(FP8X4), scales=xs[:], in_=xg[:])

@@ -20,6 +20,7 @@ ND = 8
 SORT_FROM = 6
 NS = KG - SORT_FROM
 VEC_BANKS = (3, 7)
+VEC_BANKS_ODD = (7,)
 FLOPS = 2 * 2 * B * K * N
 
 
@@ -139,12 +140,13 @@ def tile_optimizedlinear_w_kernel(
             g_words = g_sb[:].bitcast(F32)
             srt = spool.tile([P, 2 * NS * 256], F32, name="srt", tag="srt")
             sorted_words[d] = srt
-            for s in range(2):
-                first = s * row_words + 256 * (SORT_FROM - first_pass)
-                nc.vector.tensor_copy(
-                    out=srt[:, NS * 256 * s : NS * 256 * (s + 1)].rearrange("p (g u c) -> p g u c", g=NS, u=2),
-                    in_=g_words[:, first : first + NS * 256].rearrange("p (g c u) -> p g u c", g=NS, u=2),
-                )
+            first = 256 * (SORT_FROM - first_pass)
+            nc.vector.tensor_copy(
+                out=srt[:].rearrange("p (s u n) -> p s u n", s=2, u=2),
+                in_=g_words[:, 0 : 2 * row_words]
+                .rearrange("p (s w) -> p s w", s=2)[:, :, first : first + NS * 256]
+                .rearrange("p s (n u) -> p s u n", u=2),
+            )
 
         def transposes(hh):
             d, h = divmod(hh, 2)
@@ -162,12 +164,12 @@ def tile_optimizedlinear_w_kernel(
                             first = s * row_words + 256 * (g - first_pass) + u
                             block = g_words[:, first : first + 255 : 2]
                         else:
-                            first = NS * 256 * s + 256 * (g - SORT_FROM) + 128 * u
+                            first = ((2 * s + u) * NS + g - SORT_FROM) * 128
                             block = sorted_words[d][:, first : first + 128]
                         nc.tensor.transpose(bank[:, 2 * s + u, :], block, ident[:])
                 dst = gr_words[:, 512 * gl : 512 * (gl + 1)].rearrange("p (i c) -> p i c", c=4)
                 src = bank[:].rearrange("p c i -> p i c")
-                if g not in VEC_BANKS:
+                if g not in (VEC_BANKS if d % 2 == 0 else VEC_BANKS_ODD):
                     nc.scalar.copy(out=dst, in_=src)
                 else:
                     nc.vector.tensor_copy(out=dst, in_=src)

@@ -64,9 +64,9 @@ def tile_optimizedlinear_w_kernel(
         g_tiles = {}
 
         def load_scale_rows(h, q):
-            nc.sync.dma_start(
-                out=planes[32 * q : 32 * q + 16, h, :].bitcast(I32),
-                in_=weight_scales[4 * h : 4 * h + 4, 4 * q : 4 * q + 4, :].bitcast(I32),
+            nc.scalar.dma_start(
+                out=planes[32 * q : 32 * q + 16, h, :].bitcast(F32),
+                in_=weight_scales[4 * h : 4 * h + 4, 4 * q : 4 * q + 4, :].bitcast(F32),
             )
 
         def load_g(d):
@@ -84,8 +84,9 @@ def tile_optimizedlinear_w_kernel(
                     g_tiles[(d, h)] = (g_sb, K // 2, 0)
                 nc.sync.dma_start(out=g_sb[:], in_=g_rows[d])
             if 3 <= d <= 6:
-                for j in (2 * (d - 3), 2 * (d - 3) + 1):
-                    load_scale_rows(j // 4, j % 4)
+                h, pair = divmod(d - 3, 2)
+                load_scale_rows(h, pair)
+                load_scale_rows(h, pair + 2)
 
         for d in range(3):
             load_g(d)

@@ -17,10 +17,10 @@ K = 4096
 N = 2048
 KG = K // 512
 ND = 8
-SORT_FROM = 6
-NS = KG - SORT_FROM
-VEC_BANKS = (3, 7)
-VEC_BANKS_ODD = (7,)
+NU = 2 * ND
+SORTED_FROM = 2
+LOOK = 2
+SPLIT_BLOCKS = 2
 FLOPS = 2 * 2 * B * K * N
 
 
@@ -33,7 +33,7 @@ def tile_optimizedlinear_w_kernel(
         graw = ctx.enter_context(tc.tile_pool(name="graw", bufs=4))
         grp = ctx.enter_context(tc.tile_pool(name="grp", bufs=3))
         cod = ctx.enter_context(tc.tile_pool(name="cod", bufs=6))
-        spool = ctx.enter_context(tc.tile_pool(name="spool", bufs=2))
+        spool = ctx.enter_context(tc.tile_pool(name="spool", bufs=4))
         wpool = ctx.enter_context(tc.tile_pool(name="wpool", bufs=1))
         ps_t = ctx.enter_context(tc.psum_pool(name="ps_t", bufs=6))
         ps_p = ctx.enter_context(tc.psum_pool(name="ps_p", bufs=2))
@@ -70,7 +70,7 @@ def tile_optimizedlinear_w_kernel(
             )
 
         def load_g(d):
-            if d == 0:
+            if d < SPLIT_BLOCKS:
                 for h in range(2):
                     g_half = graw.tile([P, K], BF16, name="g_half", tag="g_sb")
                     g_tiles[(d, h)] = (g_half, K // 4, 4 * h)
@@ -88,7 +88,7 @@ def tile_optimizedlinear_w_kernel(
                 load_scale_rows(h, pair)
                 load_scale_rows(h, pair + 2)
 
-        for d in range(3):
+        for d in range(SPLIT_BLOCKS):
             load_g(d)
 
         w_tiles = {}
@@ -136,16 +136,17 @@ def tile_optimizedlinear_w_kernel(
 
         sorted_words = {}
 
-        def sort_words(d):
-            g_sb, row_words, first_pass = g_tiles[(d, 1)]
-            g_words = g_sb[:].bitcast(F32)
-            srt = spool.tile([P, 2 * NS * 256], F32, name="srt", tag="srt")
-            sorted_words[d] = srt
-            first = 256 * (SORT_FROM - first_pass)
+        def sort_words(hh):
+            d, h = divmod(hh, 2)
+            g_sb, row_words, first_pass = g_tiles[(d, h)]
+            srt = spool.tile([P, 1024], F32, name="srt", tag="srt")
+            sorted_words[hh] = srt
+            first = 256 * (4 * h + SORTED_FROM - first_pass)
             nc.vector.tensor_copy(
                 out=srt[:].rearrange("p (s u n) -> p s u n", s=2, u=2),
-                in_=g_words[:, 0 : 2 * row_words]
-                .rearrange("p (s w) -> p s w", s=2)[:, :, first : first + NS * 256]
+                in_=g_sb[:]
+                .bitcast(F32)
+                .rearrange("p (s w) -> p s w", s=2)[:, :, first : first + 512]
                 .rearrange("p s (n u) -> p s u n", u=2),
             )
 
@@ -161,19 +162,16 @@ def tile_optimizedlinear_w_kernel(
                 bank = ps_t.tile([P, 4, P], F32, name="bank", tag="t")
                 for s in range(2):
                     for u in range(2):
-                        if g < SORT_FROM:
+                        if gl < SORTED_FROM:
                             first = s * row_words + 256 * (g - first_pass) + u
                             block = g_words[:, first : first + 255 : 2]
                         else:
-                            first = ((2 * s + u) * NS + g - SORT_FROM) * 128
-                            block = sorted_words[d][:, first : first + 128]
+                            first = (2 * s + u) * 256 + (gl - SORTED_FROM) * 128
+                            block = sorted_words[hh][:, first : first + 128]
                         nc.tensor.transpose(bank[:, 2 * s + u, :], block, ident[:])
                 dst = gr_words[:, 512 * gl : 512 * (gl + 1)].rearrange("p (i c) -> p i c", c=4)
                 src = bank[:].rearrange("p c i -> p i c")
-                if g not in (VEC_BANKS if d % 2 == 0 else VEC_BANKS_ODD):
-                    nc.scalar.copy(out=dst, in_=src)
-                else:
-                    nc.vector.tensor_copy(out=dst, in_=src)
+                nc.scalar.copy(out=dst, in_=src)
 
         def quantise(hh):
             cd = cod.tile([P, 1024], U32, name="cd", tag="cd", align_bytes=64)
@@ -208,15 +206,12 @@ def tile_optimizedlinear_w_kernel(
         def small_terms():
             lp = ps_t.tile([P, 512], F32, name="lp", tag="t")
             nc.tensor.matmul(lp[:, 0:64], lhsT=coef[:], rhs=pick[:], start=True, stop=True)
-            nc.vector.tensor_copy(out=lr_col[:], in_=lp[:, 0:1])
+            nc.scalar.copy(out=lr_col[:], in_=lp[:, 0:1])
             for nt in range(4):
                 cp = ps_t.tile([P, 512], F32, name="cp", tag="t")
                 cols = slice(512 * nt, 512 * (nt + 1))
                 nc.tensor.matmul(cp[:], lhsT=coef[:], rhs=rows[:, cols], start=True, stop=True)
-                if nt % 2 == 0:
-                    nc.scalar.copy(out=comb[:, cols], in_=cp[:])
-                else:
-                    nc.vector.tensor_copy(out=comb[:, cols], in_=cp[:])
+                nc.scalar.copy(out=comb[:, cols], in_=cp[:])
 
         def fold_pert(nt):
             cols = slice(512 * nt, 512 * (nt + 1))
@@ -229,17 +224,19 @@ def tile_optimizedlinear_w_kernel(
                 op1=ALU.add,
             )
 
-        for hh in range(2 * ND):
+        for hh in range(LOOK):
+            sort_words(hh)
+        for hh in range(NU):
             d, h = divmod(hh, 2)
-            if h == 0 and NS > 0:
-                sort_words(d)
             transposes(hh)
             if hh == 0:
                 nc.vector.quantize_mx(out=xq[:].bitcast(FP8X4), scales=xs[:], in_=xg[:])
             else:
                 quantise(hh - 1)
-            if hh == 0:
-                load_g(3)
+            if hh < 4:
+                load_g(hh + 2)
+            if hh + LOOK < NU:
+                sort_words(hh + LOOK)
             if h == 1:
                 if d == 0:
                     small_terms()
@@ -247,11 +244,11 @@ def tile_optimizedlinear_w_kernel(
                     pert_passes(d - 1)
                     if d % 2 == 0:
                         fold_pert((d - 2) // 2)
-                if d + 4 < ND:
+                if 2 <= d and d + 4 < ND:
                     load_g(d + 4)
                 if d + 4 == ND - 1:
                     load_w()
-        quantise(2 * ND - 1)
+        quantise(NU - 1)
 
         base = {}
         for nt in range(4):

@@ -21,6 +21,7 @@ NU = 2 * ND
 SORTED_FROM = 2
 LOOK = 2
 SPLIT_BLOCKS = 2
+COL_TILES = ((0, 512), (512, 512), (1024, 512), (1536, 256), (1792, 256))
 FLOPS = 2 * 2 * B * K * N
 
 
@@ -101,14 +102,12 @@ def tile_optimizedlinear_w_kernel(
                     out=w_sb[:].bitcast(I32),
                     in_=weight_words[g].rearrange("p n t -> p (n t)").bitcast(I32),
                 )
-            for nt in range(4):
-                w_last = wpool.tile([P, 512], U32, name="w_last%d" % nt, align_bytes=64)
-                w_tiles[(KG - 1, nt)] = w_last
+            for first, width in COL_TILES:
+                w_last = wpool.tile([P, width], U32, name="w_last%d" % first, align_bytes=64)
+                w_tiles[(KG - 1, first)] = w_last
                 nc.sync.dma_start(
                     out=w_last[:].bitcast(I32),
-                    in_=weight_words[KG - 1][:, nt * 512 : (nt + 1) * 512, :]
-                    .rearrange("p n t -> p (n t)")
-                    .bitcast(I32),
+                    in_=weight_words[KG - 1][:, first : first + width, :].rearrange("p n t -> p (n t)").bitcast(I32),
                 )
 
         x_words = x_sb[:].bitcast(F32)
@@ -251,33 +250,33 @@ def tile_optimizedlinear_w_kernel(
         quantise(NU - 1)
 
         base = {}
-        for nt in range(4):
+        for first, width in COL_TILES:
             bt = ps_t.tile([P, 512], F32, name="bt", tag="t")
-            base[nt] = bt
+            base[first] = bt
 
-        def base_pass(g, nt):
+        def base_pass(g, first, width):
             if g < KG - 1:
-                rhs = w_tiles[g][:, 512 * nt : 512 * (nt + 1)]
+                rhs = w_tiles[g][:, first : first + width]
             else:
-                rhs = w_tiles[(g, nt)][:]
+                rhs = w_tiles[(g, first)][:]
             nc.tensor.matmul_mx(
-                out=base[nt][:],
+                out=base[first][:, 0:width],
                 lhsT=xq[:, P * g : P * (g + 1)].bitcast(FP8X4),
                 lhsT_scale=xs[:, P * g : P * (g + 1)],
                 rhs=rhs.bitcast(FP8X4),
-                rhs_scale=planes[4 * (g % 4) : P, g // 4, 512 * nt : 512 * (nt + 1)],
+                rhs_scale=planes[4 * (g % 4) : P, g // 4, first : first + width],
                 start=(g == 0),
                 stop=(g == KG - 1),
             )
 
         for g in range(KG - 1):
-            for nt in range(4):
-                base_pass(g, nt)
+            for first, width in COL_TILES:
+                base_pass(g, first, width)
             if g == 1:
                 pert_passes(ND - 1)
                 fold_pert(3)
-        for nt in range(4):
-            cols = slice(512 * nt, 512 * (nt + 1))
-            base_pass(KG - 1, nt)
-            nc.vector.tensor_tensor(out=comb[:, cols], in0=base[nt][:], in1=comb[:, cols], op=ALU.subtract)
+        for first, width in COL_TILES:
+            cols = slice(first, first + width)
+            base_pass(KG - 1, first, width)
+            nc.vector.tensor_tensor(out=comb[:, cols], in0=base[first][:, 0:width], in1=comb[:, cols], op=ALU.subtract)
             nc.sync.dma_start(out=out[:, cols], in_=comb[:, cols])

@@ -170,7 +170,10 @@ def tile_optimizedlinear_w_kernel(
                         nc.tensor.transpose(bank[:, 2 * s + u, :], block, ident[:])
                 dst = gr_words[:, 512 * gl : 512 * (gl + 1)].rearrange("p (i c) -> p i c", c=4)
                 src = bank[:].rearrange("p c i -> p i c")
-                nc.scalar.copy(out=dst, in_=src)
+                if gl == 0 and h == 1:
+                    nc.vector.tensor_copy(out=dst, in_=src)
+                else:
+                    nc.scalar.copy(out=dst, in_=src)
 
         def quantise(hh):
             cd = cod.tile([P, 1024], U32, name="cd", tag="cd", align_bytes=64)

@@ -21,6 +21,7 @@ NU = 2 * ND
 SORTED_FROM = 2
 LOOK = 2
 SPLIT_BLOCKS = 2
+TAIL = KG - 2
 COL_TILES = ((0, 512), (512, 512), (1024, 512), (1536, 256), (1792, 256))
 FLOPS = 2 * 2 * B * K * N
 
@@ -95,7 +96,7 @@ def tile_optimizedlinear_w_kernel(
         w_tiles = {}
 
         def load_w():
-            for g in range(KG - 1):
+            for g in range(TAIL):
                 w_sb = wpool.tile([P, N], U32, name="w_sb%d" % g, align_bytes=64)
                 w_tiles[g] = w_sb
                 nc.sync.dma_start(
@@ -103,11 +104,13 @@ def tile_optimizedlinear_w_kernel(
                     in_=weight_words[g].rearrange("p n t -> p (n t)").bitcast(I32),
                 )
             for first, width in COL_TILES:
-                w_last = wpool.tile([P, width], U32, name="w_last%d" % first, align_bytes=64)
-                w_tiles[(KG - 1, first)] = w_last
+                w_last = wpool.tile([P, KG - TAIL, width], U32, name="w_last%d" % first, align_bytes=64)
+                w_tiles[(TAIL, first)] = w_last
                 nc.sync.dma_start(
                     out=w_last[:].bitcast(I32),
-                    in_=weight_words[KG - 1][:, first : first + width, :].rearrange("p n t -> p (n t)").bitcast(I32),
+                    in_=weight_words[TAIL:KG, :, first : first + width, :]
+                    .rearrange("g p n t -> p g (n t)")
+                    .bitcast(I32),
                 )
 
         x_words = x_sb[:].bitcast(F32)
@@ -258,10 +261,10 @@ def tile_optimizedlinear_w_kernel(
             base[first] = bt
 
         def base_pass(g, first, width):
-            if g < KG - 1:
+            if g < TAIL:
                 rhs = w_tiles[g][:, first : first + width]
             else:
-                rhs = w_tiles[(g, first)][:]
+                rhs = w_tiles[(TAIL, first)][:, g - TAIL, :]
             nc.tensor.matmul_mx(
                 out=base[first][:, 0:width],
                 lhsT=xq[:, P * g : P * (g + 1)].bitcast(FP8X4),
@@ -272,7 +275,7 @@ def tile_optimizedlinear_w_kernel(
                 stop=(g == KG - 1),
             )
 
-        for g in range(KG - 1):
+        for g in range(TAIL):
             for first, width in COL_TILES:
                 base_pass(g, first, width)
             if g == 1:
@@ -280,6 +283,7 @@ def tile_optimizedlinear_w_kernel(
                 fold_pert(3)
         for first, width in COL_TILES:
             cols = slice(first, first + width)
-            base_pass(KG - 1, first, width)
+            for g in range(TAIL, KG):
+                base_pass(g, first, width)
             nc.vector.tensor_tensor(out=comb[:, cols], in0=base[first][:, 0:width], in1=comb[:, cols], op=ALU.subtract)
             nc.sync.dma_start(out=out[:, cols], in_=comb[:, cols])

from contextlib import ExitStack

import concourse.mybir as mybir
from concourse.masks import make_identity

F32 = mybir.dt.float32
BF16 = mybir.dt.bfloat16
U32 = mybir.dt.uint32
U8 = mybir.dt.uint8
I32 = mybir.dt.int32
FP8X4 = mybir.dt.float8_e4m3fn_x4
ALU = mybir.AluOpType

P = 128
B = 128
K = 4096
N = 2048
KG = K // 512
ND = 8
NU = 2 * ND
SORTED_FROM = 2
LOOK = 2
SPLIT_BLOCKS = 2
TAIL = KG - 2
COL_TILES = ((0, 512), (512, 512), (1024, 512), (1536, 256), (1792, 256))
FLOPS = 2 * 2 * B * K * N


def tile_optimizedlinear_w_kernel(
    tc, input_data, weight_words, weight_scales, bias, prev_grad, prev_bias_grad, lr_samples, out
):
    nc = tc.nc
    with ExitStack() as ctx:
        const = ctx.enter_context(tc.tile_pool(name="const", bufs=1))
        graw = ctx.enter_context(tc.tile_pool(name="graw", bufs=4))
        grp = ctx.enter_context(tc.tile_pool(name="grp", bufs=3))
        cod = ctx.enter_context(tc.tile_pool(name="cod", bufs=6))
        spool = ctx.enter_context(tc.tile_pool(name="spool", bufs=4))
        wpool = ctx.enter_context(tc.tile_pool(name="wpool", bufs=1))
        ps_t = ctx.enter_context(tc.psum_pool(name="ps_t", bufs=6))
        ps_p = ctx.enter_context(tc.psum_pool(name="ps_p", bufs=2))
        ctx.enter_context(tc.manual_schedule())

        ident = const.tile([P, P], F32, name="ident")
        make_identity(nc, ident[:])
        coef = const.tile([P, P], BF16, name="coef")
        nc.vector.memset(coef[:], 0.0)
        nc.vector.memset(coef[32:64, :], -1.0)
        rows = const.tile([P, N], BF16, name="rows")
        nc.vector.memset(rows[:], 0.0)
        pick = const.tile([P, 64], BF16, name="pick")
        nc.vector.memset(pick[:], 0.0)
        nc.vector.memset(pick[0:32, :], 1.0)
        planes = const.tile([P, 2, N], U8, name="planes", align_bytes=64)
        nc.vector.memset(planes[:].rearrange("p h n -> p (h n)").bitcast(I32), 0)
        nc.scalar.dma_start(out=coef[0:1, :], in_=lr_samples.rearrange("(o b) -> o b", o=1))
        nc.scalar.dma_start(out=rows[0:1, :], in_=prev_bias_grad.rearrange("(o n) -> o n", o=1))
        nc.scalar.dma_start(out=rows[32:33, :], in_=bias.rearrange("(o n) -> o n", o=1))

        x_sb = const.tile([P, K], BF16, name="x_sb")
        nc.sync.dma_start(out=x_sb[:, 0 : K // 2], in_=input_data[:, 0 : K // 2])
        nc.sync.dma_start(out=x_sb[:, K // 2 : K], in_=input_data[:, K // 2 : K])

        g_rows = prev_grad.rearrange("(d i s) k -> d i (s k)", i=P, s=2)
        g_split = prev_grad.rearrange("(d i s) k -> d i s k", i=P, s=2)
        g_tiles = {}

        def load_scale_rows(h, q):
            nc.scalar.dma_start(
                out=planes[32 * q : 32 * q + 16, h, :].bitcast(F32),
                in_=weight_scales[4 * h : 4 * h + 4, 4 * q : 4 * q + 4, :].bitcast(F32),
            )

        def load_g(d):
            if d < SPLIT_BLOCKS:
                for h in range(2):
                    g_half = graw.tile([P, K], BF16, name="g_half", tag="g_sb")
                    g_tiles[(d, h)] = (g_half, K // 4, 4 * h)
                    nc.sync.dma_start(
                        out=g_half[:].rearrange("p (s k) -> p s k", s=2),
                        in_=g_split[d][:, :, h * (K // 2) : (h + 1) * (K // 2)],
                    )
            else:
                g_sb = graw.tile([P, 2 * K], BF16, name="g_sb", tag="g_sb")
                for h in range(2):
                    g_tiles[(d, h)] = (g_sb, K // 2, 0)
                nc.sync.dma_start(out=g_sb[:], in_=g_rows[d])
            if 3 <= d <= 6:
                h, pair = divmod(d - 3, 2)
                load_scale_rows(h, pair)
                load_scale_rows(h, pair + 2)

        for d in range(SPLIT_BLOCKS):
            load_g(d)

        w_tiles = {}

        def load_w():
            for g in range(TAIL):
                w_sb = wpool.tile([P, N], U32, name="w_sb%d" % g, align_bytes=64)
                w_tiles[g] = w_sb
                nc.sync.dma_start(
                    out=w_sb[:].bitcast(I32),
                    in_=weight_words[g].rearrange("p n t -> p (n t)").bitcast(I32),
                )
            for first, width in COL_TILES:
                w_last = wpool.tile([P, KG - TAIL, width], U32, name="w_last%d" % first, align_bytes=64)
                w_tiles[(TAIL, first)] = w_last
                nc.sync.dma_start(
                    out=w_last[:].bitcast(I32),
                    in_=weight_words[TAIL:KG, :, first : first + width, :]
                    .rearrange("g p n t -> p g (n t)")
                    .bitcast(I32),
                )

        x_words = x_sb[:].bitcast(F32)
        xg = const.tile([P, K], BF16, name="xg", align_bytes=64)
        xg_words = xg[:].bitcast(F32)
        for b in range(4):
            xt = ps_t.tile([P, 4, P], F32, name="xt", tag="t")
            for g2 in range(2):
                g = 2 * b + g2
                for u in range(2):
                    nc.tensor.transpose(
                        xt[:, 2 * g2 + u, :], x_words[:, 256 * g + u : 256 * (g + 1) : 2], ident[:]
                    )
            dst = xg_words[:, 512 * b : 512 * (b + 1)].rearrange("p (g r u) -> p g r u", g=2, u=2)
            src = xt[:].rearrange("p (g u) r -> p g r u", g=2)
            if b % 2 == 0:
                nc.scalar.copy(out=dst, in_=src)
            else:
                nc.vector.tensor_copy(out=dst, in_=src)
        xq = const.tile([P, K // 4], U32, name="xq", align_bytes=64)
        xs = const.tile([P, K // 4], U8, name="xs", align_bytes=64)

        grouped = {}
        codes = {}

        sorted_words = {}

        def sort_words(hh):
            d, h = divmod(hh, 2)
            g_sb, row_words, first_pass = g_tiles[(d, h)]
            srt = spool.tile([P, 1024], F32, name="srt", tag="srt")
            sorted_words[hh] = srt
            first = 256 * (4 * h + SORTED_FROM - first_pass)
            nc.vector.tensor_copy(
                out=srt[:].rearrange("p (s u n) -> p s u n", s=2, u=2),
                in_=g_sb[:]
                .bitcast(F32)
                .rearrange("p (s w) -> p s w", s=2)[:, :, first : first + 512]
                .rearrange("p s (n u) -> p s u n", u=2),
            )

        def transposes(hh):
            d, h = divmod(hh, 2)
            g_sb, row_words, first_pass = g_tiles[(d, h)]
            g_words = g_sb[:].bitcast(F32)
            gr = grp.tile([P, 4096], BF16, name="gr", tag="gr", align_bytes=64)
            grouped[hh] = gr
            gr_words = gr[:].bitcast(F32)
            for gl in range(4):
                g = 4 * h + gl
                bank = ps_t.tile([P, 4, P], F32, name="bank", tag="t")
                for s in range(2):
                    for u in range(2):
                        if gl < SORTED_FROM:
                            first = s * row_words + 256 * (g - first_pass) + u
                            block = g_words[:, first : first + 255 : 2]
                        else:
                            first = (2 * s + u) * 256 + (gl - SORTED_FROM) * 128
                            block = sorted_words[hh][:, first : first + 128]
                        nc.tensor.transpose(bank[:, 2 * s + u, :], block, ident[:])
                dst = gr_words[:, 512 * gl : 512 * (gl + 1)].rearrange("p (i c) -> p i c", c=4)
                src = bank[:].rearrange("p c i -> p i c")
                if gl == 0 and h == 1:
                    nc.vector.tensor_copy(out=dst, in_=src)
                else:
                    nc.scalar.copy(out=dst, in_=src)

        def quantise(hh):
            cd = cod.tile([P, 1024], U32, name="cd", tag="cd", align_bytes=64)
            sc = cod.tile([P, 1024], U8, name="sc", tag="sc", align_bytes=64)
            codes[hh] = (cd, sc)
            nc.vector.quantize_mx(out=cd[:].bitcast(FP8X4), scales=sc[:], in_=grouped[hh][:])

        pert = {}

        def pert_passes(d):
            nt, half = divmod(d, 2)
            if half == 0:
                acc = ps_p.tile([P, 512], F32, name="acc", tag="acc")
                pert[nt] = acc
            acc = pert[nt]
            for g in range(KG):
                cd, sc = codes[2 * d + g // 4]
                cols = slice(256 * (g % 4), 256 * (g % 4) + 256)
                nc.tensor.matmul_mx(
                    out=acc[:, 256 * half : 256 * half + 256],
                    lhsT=xq[:, P * g : P * (g + 1)].bitcast(FP8X4),
                    lhsT_scale=xs[:, P * g : P * (g + 1)],
                    rhs=cd[:, cols].bitcast(FP8X4),
                    rhs_scale=sc[:, cols],
                    start=(g == 0),
                    stop=(g == KG - 1),
                )

        comb = const.tile([P, N], F32, name="comb")
        lr_col = const.tile([P, 1], F32, name="lr_col")

        def small_terms():
            lp = ps_t.tile([P, 512], F32, name="lp", tag="t")
            nc.tensor.matmul(lp[:, 0:64], lhsT=coef[:], rhs=pick[:], start=True, stop=True)
            nc.scalar.copy(out=lr_col[:], in_=lp[:, 0:1])
            for nt in range(4):
                cp = ps_t.tile([P, 512], F32, name="cp", tag="t")
                cols = slice(512 * nt, 512 * (nt + 1))
                nc.tensor.matmul(cp[:], lhsT=coef[:], rhs=rows[:, cols], start=True, stop=True)
                nc.scalar.copy(out=comb[:, cols], in_=cp[:])

        def fold_pert(nt):
            cols = slice(512 * nt, 512 * (nt + 1))
            nc.vector.scalar_tensor_tensor(
                out=comb[:, cols],
                in0=pert[nt][:],
                scalar=lr_col[:, 0:1],
                in1=comb[:, cols],
                op0=ALU.mult,
                op1=ALU.add,
            )

        for hh in range(LOOK):
            sort_words(hh)
        for hh in range(NU):
            d, h = divmod(hh, 2)
            transposes(hh)
            if hh == 0:
                nc.vector.quantize_mx(out=xq[:].bitcast(FP8X4), scales=xs[:], in_=xg[:])
            else:
                quantise(hh - 1)
            if hh < 4:
                load_g(hh + 2)
            if hh + LOOK < NU:
                sort_words(hh + LOOK)
            if h == 1:
                if d == 0:
                    small_terms()
                else:
                    pert_passes(d - 1)
                    if d % 2 == 0:
                        fold_pert((d - 2) // 2)
                if 2 <= d and d + 4 < ND:
                    load_g(d + 4)
                if d + 4 == ND - 1:
                    load_w()
        quantise(NU - 1)

        base = {}
        for first, width in COL_TILES:
            bt = ps_t.tile([P, 512], F32, name="bt", tag="t")
            base[first] = bt

        def base_pass(g, first, width):
            if g < TAIL:
                rhs = w_tiles[g][:, first : first + width]
            else:
                rhs = w_tiles[(TAIL, first)][:, g - TAIL, :]
            nc.tensor.matmul_mx(
                out=base[first][:, 0:width],
                lhsT=xq[:, P * g : P * (g + 1)].bitcast(FP8X4),
                lhsT_scale=xs[:, P * g : P * (g + 1)],
                rhs=rhs.bitcast(FP8X4),
                rhs_scale=planes[4 * (g % 4) : P, g // 4, first : first + width],
                start=(g == 0),
                stop=(g == KG - 1),
            )

        for g in range(TAIL):
            for first, width in COL_TILES:
                base_pass(g, first, width)
            if g == 1:
                pert_passes(ND - 1)
                fold_pert(3)
        for first, width in COL_TILES:
            cols = slice(first, first + width)
            for g in range(TAIL, KG):
                base_pass(g, first, width)
            nc.vector.tensor_tensor(out=comb[:, cols], in0=base[first][:, 0:width], in1=comb[:, cols], op=ALU.subtract)
            nc.sync.dma_start(out=out[:, cols], in_=comb[:, cols])
